import numpy as np
import ml_dtypes

BF16 = ml_dtypes.bfloat16


def bf(x):
    return np.asarray(x, np.float32).astype(BF16)


def f32(x):
    return np.asarray(x, np.float32)


def f64(x):
    return np.asarray(x).astype(np.float64)


def striped(idx):
    return np.tile(idx.reshape(-1, 16).T, (8, 1))


H, V, N = 256, 1024, 2048


def setup_inputs():
    return {"z": f32(np.random.standard_normal((H, N))), "embed": f32(np.random.standard_normal((H, V)) / np.sqrt(H)), "ctx_b": f32(0.1 * np.random.standard_normal((H, 1))), "lm_head": bf(0.02 * np.random.standard_normal((H, V))), "offs": striped(np.random.permutation(np.tile(np.arange(V), 2))[:N])}


def reference(z, embed, ctx_b, lm_head, offs):
    idx = offs[:16].T.reshape(-1)
    zn = np.sqrt(H) * f64(embed)[:, idx] + f64(z) + f64(ctx_b)
    return f64(lm_head).T @ zn

@@ -1,0 +1,70 @@
+import concourse.mybir as mybir
+
+F32, BF16, U16 = mybir.dt.float32, mybir.dt.bfloat16, mybir.dt.uint16
+ADD = mybir.AluOpType.add
+IDENTITY = mybir.ActivationFunctionType.Identity
+
+P = 128
+H, V, N = 256, 1024, 2048
+CHANNEL_BLOCKS = H // P
+VOCAB_BLOCKS = V // P
+PIECE = 512
+PIECES = N // PIECE
+EMBED_SCALE = 16.0
+
+FLOPS = 2 * H * V * N
+
+
+def tile_trm_mor_inner_kernel(tc, z, embed, ctx_b, lm_head, offs, out):
+    nc = tc.nc
+    with (
+        tc.tile_pool(name="held", bufs=1) as held,
+        tc.tile_pool(name="sums", bufs=4) as sums_pool,
+        tc.tile_pool(name="states", bufs=4) as states_pool,
+        tc.tile_pool(name="staged", bufs=8) as staged_pool,
+        tc.psum_pool(name="psum", bufs=8) as psum_pool,
+    ):
+        offsets = held.tile([P, N // 16], U16, name="offsets")
+        nc.sync.dma_start(offsets[:], offs)
+        table, latent, context, head = [], [], [], []
+        for k in range(CHANNEL_BLOCKS):
+            rows = slice(k * P, (k + 1) * P)
+            latent.append(held.tile([P, N], F32, name=f"latent{k}"))
+            nc.sync.dma_start(latent[k][:, 0:PIECE], z[rows, 0:PIECE])
+            table.append(held.tile([P, V], F32, name=f"table{k}"))
+            nc.sync.dma_start(table[k][:], embed[rows, :])
+        for k in range(CHANNEL_BLOCKS):
+            rows = slice(k * P, (k + 1) * P)
+            context.append(held.tile([P, 1], F32, name=f"context{k}"))
+            nc.sync.dma_start(context[k][:], ctx_b[rows, :])
+            head.append(held.tile([P, V], BF16, name=f"head{k}"))
+            nc.sync.dma_start(head[k][:], lm_head[rows, :])
+        for j in range(1, PIECES):
+            tokens = slice(j * PIECE, (j + 1) * PIECE)
+            for k in range(CHANNEL_BLOCKS):
+                nc.sync.dma_start(latent[k][:, tokens], z[k * P : (k + 1) * P, tokens])
+
+        for j in range(PIECES):
+            tokens = slice(j * PIECE, (j + 1) * PIECE)
+            piece_offsets = offsets[:, j * (PIECE // 16) : (j + 1) * (PIECE // 16)]
+            state = []
+            for k in range(CHANNEL_BLOCKS):
+                shrunk = sums_pool.tile([P, PIECE], F32, name="shrunk")
+                nc.gpsimd.tensor_scalar_mul(shrunk[:], latent[k][:, tokens], 1.0 / EMBED_SCALE)
+                summed = sums_pool.tile([P, PIECE], F32, name="summed")
+                nc.vector.tensor_tensor(summed[:], table[k][:].indirect(piece_offsets), shrunk[:], ADD)
+                state.append(states_pool.tile([P, PIECE], BF16, name="state"))
+                nc.scalar.activation(state[k][:], summed[:], IDENTITY, bias=context[k][:], scale=EMBED_SCALE)
+            for v in range(VOCAB_BLOCKS):
+                words = slice(v * P, (v + 1) * P)
+                logits = psum_pool.tile([P, PIECE], F32, name="logits")
+                for k in range(CHANNEL_BLOCKS):
+                    nc.tensor.matmul(
+                        logits[:], head[k][:, words], state[k][:], start=(k == 0), stop=(k == CHANNEL_BLOCKS - 1)
+                    )
+                staged = staged_pool.tile([P, PIECE], F32, name="staged")
+                if v % 3 == 0:
+                    nc.vector.tensor_copy(staged[:], logits[:])
+                else:
+                    nc.scalar.copy(staged[:], logits[:])
+                nc.sync.dma_start(out[words, tokens], staged[:])

@@ -50,7 +50,7 @@ def tile_trm_mor_inner_kernel(tc, z, embed, ctx_b, lm_head, offs, out):
             state = []
             for k in range(CHANNEL_BLOCKS):
                 shrunk = sums_pool.tile([P, PIECE], F32, name="shrunk")
-                nc.gpsimd.tensor_scalar_mul(shrunk[:], latent[k][:, tokens], 1.0 / EMBED_SCALE)
+                nc.vector.tensor_scalar_mul(shrunk[:], latent[k][:, tokens], 1.0 / EMBED_SCALE)
                 summed = sums_pool.tile([P, PIECE], F32, name="summed")
                 nc.vector.tensor_tensor(summed[:], table[k][:].indirect(piece_offsets), shrunk[:], ADD)
                 state.append(states_pool.tile([P, PIECE], BF16, name="state"))

@@ -1,8 +1,7 @@
 import concourse.mybir as mybir
 
 F32, BF16, U16 = mybir.dt.float32, mybir.dt.bfloat16, mybir.dt.uint16
-ADD = mybir.AluOpType.add
-IDENTITY = mybir.ActivationFunctionType.Identity
+MULT, ADD = mybir.AluOpType.mult, mybir.AluOpType.add
 
 P = 128
 H, V, N = 256, 1024, 2048
@@ -54,7 +53,7 @@ def tile_trm_mor_inner_kernel(tc, z, embed, ctx_b, lm_head, offs, out):
                 summed = sums_pool.tile([P, PIECE], F32, name="summed")
                 nc.vector.tensor_tensor(summed[:], table[k][:].indirect(piece_offsets), shrunk[:], ADD)
                 state.append(states_pool.tile([P, PIECE], BF16, name="state"))
-                nc.scalar.activation(state[k][:], summed[:], IDENTITY, bias=context[k][:], scale=EMBED_SCALE)
+                nc.vector.tensor_scalar(state[k][:], summed[:], EMBED_SCALE, context[k][:], MULT, ADD)
             for v in range(VOCAB_BLOCKS):
                 words = slice(v * P, (v + 1) * P)
                 logits = psum_pool.tile([P, PIECE], F32, name="logits")
@@ -63,7 +62,7 @@ def tile_trm_mor_inner_kernel(tc, z, embed, ctx_b, lm_head, offs, out):
                         logits[:], head[k][:, words], state[k][:], start=(k == 0), stop=(k == CHANNEL_BLOCKS - 1)
                     )
                 staged = staged_pool.tile([P, PIECE], F32, name="staged")
-                if v % 3 == 0:
+                if v == VOCAB_BLOCKS - 1:
                     nc.vector.tensor_copy(staged[:], logits[:])
                 else:
                     nc.scalar.copy(staged[:], logits[:])

@@ -9,6 +9,7 @@ CHANNEL_BLOCKS = H // P
 VOCAB_BLOCKS = V // P
 PIECE = 512
 PIECES = N // PIECE
+GROUP = 4
 EMBED_SCALE = 16.0
 
 FLOPS = 2 * H * V * N
@@ -20,7 +21,7 @@ def tile_trm_mor_inner_kernel(tc, z, embed, ctx_b, lm_head, offs, out):
         tc.tile_pool(name="held", bufs=1) as held,
         tc.tile_pool(name="sums", bufs=4) as sums_pool,
         tc.tile_pool(name="states", bufs=4) as states_pool,
-        tc.tile_pool(name="staged", bufs=8) as staged_pool,
+        tc.tile_pool(name="staged", bufs=4) as staged_pool,
         tc.psum_pool(name="psum", bufs=8) as psum_pool,
     ):
         offsets = held.tile([P, N // 16], U16, name="offsets")
@@ -32,16 +33,12 @@ def tile_trm_mor_inner_kernel(tc, z, embed, ctx_b, lm_head, offs, out):
             nc.sync.dma_start(latent[k][:, 0:PIECE], z[rows, 0:PIECE])
             table.append(held.tile([P, V], F32, name=f"table{k}"))
             nc.sync.dma_start(table[k][:], embed[rows, :])
-        for k in range(CHANNEL_BLOCKS):
-            rows = slice(k * P, (k + 1) * P)
             context.append(held.tile([P, 1], F32, name=f"context{k}"))
             nc.sync.dma_start(context[k][:], ctx_b[rows, :])
             head.append(held.tile([P, V], BF16, name=f"head{k}"))
             nc.sync.dma_start(head[k][:], lm_head[rows, :])
-        for j in range(1, PIECES):
-            tokens = slice(j * PIECE, (j + 1) * PIECE)
-            for k in range(CHANNEL_BLOCKS):
-                nc.sync.dma_start(latent[k][:, tokens], z[k * P : (k + 1) * P, tokens])
+        for k in range(CHANNEL_BLOCKS):
+            nc.sync.dma_start(latent[k][:, PIECE:N], z[k * P : (k + 1) * P, PIECE:N])
 
         for j in range(PIECES):
             tokens = slice(j * PIECE, (j + 1) * PIECE)
@@ -54,16 +51,23 @@ def tile_trm_mor_inner_kernel(tc, z, embed, ctx_b, lm_head, offs, out):
                 nc.vector.tensor_tensor(summed[:], table[k][:].indirect(piece_offsets), shrunk[:], ADD)
                 state.append(states_pool.tile([P, PIECE], BF16, name="state"))
                 nc.vector.tensor_scalar(state[k][:], summed[:], EMBED_SCALE, context[k][:], MULT, ADD)
-            for v in range(VOCAB_BLOCKS):
-                words = slice(v * P, (v + 1) * P)
-                logits = psum_pool.tile([P, PIECE], F32, name="logits")
+            for first in range(0, VOCAB_BLOCKS, GROUP):
+                group = range(first, first + GROUP)
+                logits = [psum_pool.tile([P, PIECE], F32, name="logits") for v in group]
                 for k in range(CHANNEL_BLOCKS):
-                    nc.tensor.matmul(
-                        logits[:], head[k][:, words], state[k][:], start=(k == 0), stop=(k == CHANNEL_BLOCKS - 1)
-                    )
-                staged = staged_pool.tile([P, PIECE], F32, name="staged")
-                if v == VOCAB_BLOCKS - 1:
-                    nc.vector.tensor_copy(staged[:], logits[:])
-                else:
-                    nc.scalar.copy(staged[:], logits[:])
-                nc.sync.dma_start(out[words, tokens], staged[:])
+                    for v in group:
+                        nc.tensor.matmul(
+                            logits[v - first][:],
+                            head[k][:, v * P : (v + 1) * P],
+                            state[k][:],
+                            start=(k == 0),
+                            stop=(k == CHANNEL_BLOCKS - 1),
+                        )
+                staged = staged_pool.tile([P, GROUP, PIECE], F32, name="staged")
+                for v in group:
+                    if v == VOCAB_BLOCKS - 1:
+                        nc.vector.tensor_copy(staged[:, v - first, :], logits[v - first][:])
+                    else:
+                        nc.scalar.copy(staged[:, v - first, :], logits[v - first][:])
+                group_rows = out[first * P : (first + GROUP) * P, tokens]
+                nc.sync.dma_start(group_rows.rearrange("(g p) t -> p g t", p=P), staged[:])

@@ -9,7 +9,7 @@ CHANNEL_BLOCKS = H // P
 VOCAB_BLOCKS = V // P
 PIECE = 512
 PIECES = N // PIECE
-GROUP = 4
+PAIR = 2
 EMBED_SCALE = 16.0
 
 FLOPS = 2 * H * V * N
@@ -21,7 +21,7 @@ def tile_trm_mor_inner_kernel(tc, z, embed, ctx_b, lm_head, offs, out):
         tc.tile_pool(name="held", bufs=1) as held,
         tc.tile_pool(name="sums", bufs=4) as sums_pool,
         tc.tile_pool(name="states", bufs=4) as states_pool,
-        tc.tile_pool(name="staged", bufs=4) as staged_pool,
+        tc.tile_pool(name="staged", bufs=8) as staged_pool,
         tc.psum_pool(name="psum", bufs=8) as psum_pool,
     ):
         offsets = held.tile([P, N // 16], U16, name="offsets")
@@ -33,12 +33,16 @@ def tile_trm_mor_inner_kernel(tc, z, embed, ctx_b, lm_head, offs, out):
             nc.sync.dma_start(latent[k][:, 0:PIECE], z[rows, 0:PIECE])
             table.append(held.tile([P, V], F32, name=f"table{k}"))
             nc.sync.dma_start(table[k][:], embed[rows, :])
+        for k in range(CHANNEL_BLOCKS):
+            rows = slice(k * P, (k + 1) * P)
             context.append(held.tile([P, 1], F32, name=f"context{k}"))
-            nc.sync.dma_start(context[k][:], ctx_b[rows, :])
+            nc.scalar.dma_start(context[k][:], ctx_b[rows, :])
             head.append(held.tile([P, V], BF16, name=f"head{k}"))
             nc.sync.dma_start(head[k][:], lm_head[rows, :])
-        for k in range(CHANNEL_BLOCKS):
-            nc.sync.dma_start(latent[k][:, PIECE:N], z[k * P : (k + 1) * P, PIECE:N])
+        for j in range(1, PIECES):
+            tokens = slice(j * PIECE, (j + 1) * PIECE)
+            for k in range(CHANNEL_BLOCKS):
+                nc.sync.dma_start(latent[k][:, tokens], z[k * P : (k + 1) * P, tokens])
 
         for j in range(PIECES):
             tokens = slice(j * PIECE, (j + 1) * PIECE)
@@ -51,11 +55,11 @@ def tile_trm_mor_inner_kernel(tc, z, embed, ctx_b, lm_head, offs, out):
                 nc.vector.tensor_tensor(summed[:], table[k][:].indirect(piece_offsets), shrunk[:], ADD)
                 state.append(states_pool.tile([P, PIECE], BF16, name="state"))
                 nc.vector.tensor_scalar(state[k][:], summed[:], EMBED_SCALE, context[k][:], MULT, ADD)
-            for first in range(0, VOCAB_BLOCKS, GROUP):
-                group = range(first, first + GROUP)
-                logits = [psum_pool.tile([P, PIECE], F32, name="logits") for v in group]
+            for first in range(0, VOCAB_BLOCKS, PAIR):
+                pair = range(first, first + PAIR)
+                logits = [psum_pool.tile([P, PIECE], F32, name="logits") for v in pair]
                 for k in range(CHANNEL_BLOCKS):
-                    for v in group:
+                    for v in pair:
                         nc.tensor.matmul(
                             logits[v - first][:],
                             head[k][:, v * P : (v + 1) * P],
@@ -63,11 +67,11 @@ def tile_trm_mor_inner_kernel(tc, z, embed, ctx_b, lm_head, offs, out):
                             start=(k == 0),
                             stop=(k == CHANNEL_BLOCKS - 1),
                         )
-                staged = staged_pool.tile([P, GROUP, PIECE], F32, name="staged")
-                for v in group:
+                staged = staged_pool.tile([P, PAIR, PIECE], F32, name="staged")
+                for v in pair:
                     if v == VOCAB_BLOCKS - 1:
                         nc.vector.tensor_copy(staged[:, v - first, :], logits[v - first][:])
                     else:
                         nc.scalar.copy(staged[:, v - first, :], logits[v - first][:])
-                group_rows = out[first * P : (first + GROUP) * P, tokens]
-                nc.sync.dma_start(group_rows.rearrange("(g p) t -> p g t", p=P), staged[:])
+                pair_rows = out[first * P : (first + PAIR) * P, tokens]
+                nc.sync.dma_start(pair_rows.rearrange("(g p) t -> p g t", p=P), staged[:])

@@ -69,9 +69,6 @@ def tile_trm_mor_inner_kernel(tc, z, embed, ctx_b, lm_head, offs, out):
                         )
                 staged = staged_pool.tile([P, PAIR, PIECE], F32, name="staged")
                 for v in pair:
-                    if v == VOCAB_BLOCKS - 1:
-                        nc.vector.tensor_copy(staged[:, v - first, :], logits[v - first][:])
-                    else:
-                        nc.scalar.copy(staged[:, v - first, :], logits[v - first][:])
+                    nc.scalar.copy(staged[:, v - first, :], logits[v - first][:])
                 pair_rows = out[first * P : (first + PAIR) * P, tokens]
                 nc.sync.dma_start(pair_rows.rearrange("(g p) t -> p g t", p=P), staged[:])

@@ -11,6 +11,7 @@ PIECE = 512
 PIECES = N // PIECE
 PAIR = 2
 EMBED_SCALE = 16.0
+WARM_UP = 16
 
 FLOPS = 2 * H * V * N
 
@@ -43,6 +44,12 @@ def tile_trm_mor_inner_kernel(tc, z, embed, ctx_b, lm_head, offs, out):
             tokens = slice(j * PIECE, (j + 1) * PIECE)
             for k in range(CHANNEL_BLOCKS):
                 nc.sync.dma_start(latent[k][:, tokens], z[k * P : (k + 1) * P, tokens])
+
+        ones = held.tile([P, PIECE], BF16, name="ones")
+        nc.vector.memset(ones[:], 1.0)
+        unread = psum_pool.tile([P, PIECE], F32, name="unread", tag="logits")
+        for i in range(WARM_UP):
+            nc.tensor.matmul(unread[:], ones[:, 0:P], ones[:], start=True, stop=True)
 
         for j in range(PIECES):
             tokens = slice(j * PIECE, (j + 1) * PIECE)

@@ -77,5 +77,8 @@ def tile_trm_mor_inner_kernel(tc, z, embed, ctx_b, lm_head, offs, out):
                 staged = staged_pool.tile([P, PAIR, PIECE], F32, name="staged")
                 for v in pair:
                     nc.scalar.copy(staged[:, v - first, :], logits[v - first][:])
-                pair_rows = out[first * P : (first + PAIR) * P, tokens]
-                nc.sync.dma_start(pair_rows.rearrange("(g p) t -> p g t", p=P), staged[:])
+                    if j == 0 and first == 0:
+                        nc.sync.dma_start(out[v * P : (v + 1) * P, tokens], staged[:, v - first, :])
+                if j > 0 or first > 0:
+                    pair_rows = out[first * P : (first + PAIR) * P, tokens]
+                    nc.sync.dma_start(pair_rows.rearrange("(g p) t -> p g t", p=P), staged[:])

import concourse.mybir as mybir

F32, BF16, U16 = mybir.dt.float32, mybir.dt.bfloat16, mybir.dt.uint16
MULT, ADD = mybir.AluOpType.mult, mybir.AluOpType.add

P = 128
H, V, N = 256, 1024, 2048
CHANNEL_BLOCKS = H // P
VOCAB_BLOCKS = V // P
PIECE = 512
PIECES = N // PIECE
PAIR = 2
EMBED_SCALE = 16.0
WARM_UP = 16

FLOPS = 2 * H * V * N


def tile_trm_mor_inner_kernel(tc, z, embed, ctx_b, lm_head, offs, out):
    nc = tc.nc
    with (
        tc.tile_pool(name="held", bufs=1) as held,
        tc.tile_pool(name="sums", bufs=4) as sums_pool,
        tc.tile_pool(name="states", bufs=4) as states_pool,
        tc.tile_pool(name="staged", bufs=8) as staged_pool,
        tc.psum_pool(name="psum", bufs=8) as psum_pool,
    ):
        offsets = held.tile([P, N // 16], U16, name="offsets")
        nc.sync.dma_start(offsets[:], offs)
        table, latent, context, head = [], [], [], []
        for k in range(CHANNEL_BLOCKS):
            rows = slice(k * P, (k + 1) * P)
            latent.append(held.tile([P, N], F32, name=f"latent{k}"))
            nc.sync.dma_start(latent[k][:, 0:PIECE], z[rows, 0:PIECE])
            table.append(held.tile([P, V], F32, name=f"table{k}"))
            nc.sync.dma_start(table[k][:], embed[rows, :])
        for k in range(CHANNEL_BLOCKS):
            rows = slice(k * P, (k + 1) * P)
            context.append(held.tile([P, 1], F32, name=f"context{k}"))
            nc.scalar.dma_start(context[k][:], ctx_b[rows, :])
            head.append(held.tile([P, V], BF16, name=f"head{k}"))
            nc.sync.dma_start(head[k][:], lm_head[rows, :])
        for j in range(1, PIECES):
            tokens = slice(j * PIECE, (j + 1) * PIECE)
            for k in range(CHANNEL_BLOCKS):
                nc.sync.dma_start(latent[k][:, tokens], z[k * P : (k + 1) * P, tokens])

        ones = held.tile([P, PIECE], BF16, name="ones")
        nc.vector.memset(ones[:], 1.0)
        unread = psum_pool.tile([P, PIECE], F32, name="unread", tag="logits")
        for i in range(WARM_UP):
            nc.tensor.matmul(unread[:], ones[:, 0:P], ones[:], start=True, stop=True)

        for j in range(PIECES):
            tokens = slice(j * PIECE, (j + 1) * PIECE)
            piece_offsets = offsets[:, j * (PIECE // 16) : (j + 1) * (PIECE // 16)]
            state = []
            for k in range(CHANNEL_BLOCKS):
                shrunk = sums_pool.tile([P, PIECE], F32, name="shrunk")
                nc.vector.tensor_scalar_mul(shrunk[:], latent[k][:, tokens], 1.0 / EMBED_SCALE)
                summed = sums_pool.tile([P, PIECE], F32, name="summed")
                nc.vector.tensor_tensor(summed[:], table[k][:].indirect(piece_offsets), shrunk[:], ADD)
                state.append(states_pool.tile([P, PIECE], BF16, name="state"))
                nc.vector.tensor_scalar(state[k][:], summed[:], EMBED_SCALE, context[k][:], MULT, ADD)
            for first in range(0, VOCAB_BLOCKS, PAIR):
                pair = range(first, first + PAIR)
                logits = [psum_pool.tile([P, PIECE], F32, name="logits") for v in pair]
                for k in range(CHANNEL_BLOCKS):
                    for v in pair:
                        nc.tensor.matmul(
                            logits[v - first][:],
                            head[k][:, v * P : (v + 1) * P],
                            state[k][:],
                            start=(k == 0),
                            stop=(k == CHANNEL_BLOCKS - 1),
                        )
                staged = staged_pool.tile([P, PAIR, PIECE], F32, name="staged")
                for v in pair:
                    nc.scalar.copy(staged[:, v - first, :], logits[v - first][:])
                    if j == 0 and first == 0:
                        nc.sync.dma_start(out[v * P : (v + 1) * P, tokens], staged[:, v - first, :])
                if j > 0 or first > 0:
                    pair_rows = out[first * P : (first + PAIR) * P, tokens]
                    nc.sync.dma_start(pair_rows.rearrange("(g p) t -> p g t", p=P), staged[:])
